import numpy as np
import ml_dtypes


def mxq(x, axis, fmt="e4m3"):
    dtype, down = {"e4m3": (ml_dtypes.float8_e4m3fn, 7), "e5m2": (ml_dtypes.float8_e5m2, 14)}[fmt]
    v = np.moveaxis(np.asarray(x, np.float32).astype(ml_dtypes.bfloat16).astype(np.float64), axis, -1)
    blocks = v.reshape(v.shape[:-1] + (-1, 32))
    amax = np.abs(blocks).max(-1, keepdims=True)
    byte = np.maximum(np.where(amax > 0, np.frexp(amax)[1] - 1 + 127, 0) - down, 1)
    scale = np.exp2(byte - 127.0)
    codes = (blocks / scale).astype(np.float32).astype(dtype).astype(np.float64)
    return np.moveaxis((codes * scale).reshape(v.shape), -1, axis)


WIDE = False


def mx_kscale(k):
    if not WIDE:
        return np.ones(k)
    levels = np.array([10, -10, 5, -5, 0])
    a = np.random.permutation(np.resize(levels, k // 512 * 4)).reshape(k // 512, 4)
    idx = np.arange(k)
    return np.exp2(a[idx // 512, idx % 128 // 32])


BF16 = ml_dtypes.bfloat16


def bf(x):
    return np.asarray(x, np.float32).astype(BF16)


def f64(x):
    return np.asarray(x).astype(np.float64)


B, S, D, H, DN, DR, DV, QL, KVL, LBLK = 4, 2048, 512, 4, 32, 64, 32, 512, 512, 64
DKV = DN + DV


def silu(v):
    return v / (1.0 + np.exp(-v))


def eta(t):
    m = t.reshape(t.shape[0], H, -1).max(-1)
    m = np.where(m == 0, 1e-6, m)
    return np.minimum(10.0 / m, 1.0)


def setup_inputs():
    s, t = mx_kscale(D), mx_kscale(KVL)
    amp = np.linspace(0.5, 1.5, S)[None, :, None]
    return {"x": bf(np.random.standard_normal((B, S, D)) * amp * s),
            "wkv_c": bf(np.random.standard_normal((KVL, D)) / np.sqrt(D) / s[None, :] * t[:, None]),
            "wkv_b": bf(np.random.standard_normal((H * DKV, KVL)) * 2.5 / np.sqrt(KVL) / t[None, :])}


def reference(x, wkv_c, wkv_b):
    kv_c = mxq(f64(x), 2, "e4m3") @ mxq(f64(wkv_c), 1, "e4m3").T
    kv = (mxq(kv_c, 2, "e4m3") @ mxq(f64(wkv_b), 1, "e4m3").T).reshape(B, S, H, DKV)
    k, v = silu(kv[..., :DN]), kv[..., DN:]
    return k * eta(k)[:, None, :, None], v

@@ -1,0 +1,263 @@
+from contextlib import ExitStack
+
+import concourse.mybir as mybir
+from concourse.masks import make_identity
+
+F32 = mybir.dt.float32
+BF16 = mybir.dt.bfloat16
+U32 = mybir.dt.uint32
+U8 = mybir.dt.uint8
+FP8X4 = mybir.dt.float8_e4m3fn_x4
+ACT = mybir.ActivationFunctionType
+ALU = mybir.AluOpType
+AXIS = mybir.AxisListType
+
+P = 128
+PACK = 4
+BATCHES, SEQ, D = 4, 2048, 512
+HEADS, HEAD_KEYS = 4, 32
+KEYS = HEADS * HEAD_KEYS
+ROWS = SEQ // P
+TILES = 4
+BLOCK = TILES * P
+BLOCKS_PER_BATCH = ROWS // TILES
+N_BLOCKS = BATCHES * BLOCKS_PER_BATCH
+
+FLOPS = 2 * BATCHES * SEQ * D * (D + 2 * KEYS)
+
+
+def tile_ssa_pb_t_kernel(tc, x, wkv_c, wkv_b, out_0, out_1):
+    nc = tc.nc
+    with ExitStack() as ctx:
+        keep = ctx.enter_context(tc.tile_pool(name="keep", bufs=1))
+        x_pool = ctx.enter_context(tc.tile_pool(name="x_pool", bufs=N_BLOCKS))
+        stage = ctx.enter_context(tc.tile_pool(name="stage", bufs=2))
+        key_pool = ctx.enter_context(tc.tile_pool(name="key_pool", bufs=BATCHES))
+        val_pool = ctx.enter_context(tc.tile_pool(name="val_pool", bufs=4))
+        small = ctx.enter_context(tc.tile_pool(name="small", bufs=BATCHES))
+        ps_turn = ctx.enter_context(tc.psum_pool(name="ps_turn", bufs=2))
+        ps_kvc = ctx.enter_context(tc.psum_pool(name="ps_kvc", bufs=4))
+        ps_kv = ctx.enter_context(tc.psum_pool(name="ps_kv", bufs=1))
+        ctx.enter_context(tc.manual_schedule())
+
+        x_rows = x.rearrange("b (p i) d -> b p i d", i=ROWS)
+        k_rows = out_0.rearrange("b (p i) h f -> b p i (h f)", i=ROWS)
+        v_rows = out_1.rearrange("b (p i) h f -> b p i (h f)", i=ROWS)
+
+        def rows_of(n):
+            first = (n % BLOCKS_PER_BATCH) * TILES
+            return n // BLOCKS_PER_BATCH, slice(first, first + TILES)
+
+        wc_rows = keep.tile([P, TILES, D], BF16)
+        nc.sync.dma_start(out=wc_rows[:], in_=wkv_c.rearrange("(m j) d -> m j d", j=PACK))
+        wb_rows = keep.tile([P, 2, D], BF16)
+        x_blocks = {}
+        for n in range(N_BLOCKS):
+            b, rows = rows_of(n)
+            x_block = x_pool.tile([P, TILES, D], BF16)
+            nc.sync.dma_start(out=x_block[:], in_=x_rows[b, :, rows, :])
+            x_blocks[n] = x_block
+            if n == 0:
+                nc.sync.dma_start(out=wb_rows[:], in_=wkv_b.rearrange("(r p) c -> p r c", p=P))
+
+        ident = keep.tile([P, P], F32)
+        make_identity(nc, ident[:])
+
+        zero = keep.tile([P, 1], F32)
+        nc.vector.memset(zero[:], 0.0)
+        warm = keep.tile([P, 1], F32)
+        nc.scalar.activation(out=warm[:], in_=zero[:], func=ACT.Silu)
+
+        def turn(rows_sb, grouped, copy):
+            words = rows_sb[:].bitcast(F32)
+            out_words = grouped[:].bitcast(F32).rearrange("p (t r u) -> p t r u", t=TILES, u=2)
+            for half in range(2):
+                turned = ps_turn.tile([P, 2, 2, P], F32, tag="turned")
+                for t in range(2):
+                    for u in range(2):
+                        nc.tensor.transpose(
+                            turned[:, t, u, :], words[:, 2 * half + t, u * P : (u + 1) * P], ident[:]
+                        )
+                copy(
+                    out=out_words[:, 2 * half : 2 * half + 2, :, :],
+                    in_=turned[:].rearrange("p t u r -> p t r u"),
+                )
+
+        def quantise(grouped, codes, scales):
+            nc.vector.quantize_mx(out=codes[:].bitcast(FP8X4), scales=scales[:], in_=grouped[:])
+
+        wc_grouped = keep.tile([P, BLOCK * PACK], BF16, align_bytes=64)
+        wc_codes = keep.tile([P, BLOCK], U32, align_bytes=64)
+        wc_scales = keep.tile([P, BLOCK], U8, align_bytes=64)
+        turn(wc_rows, wc_grouped, nc.scalar.copy)
+        quantise(wc_grouped, wc_codes, wc_scales)
+
+        wb_grouped = keep.tile([P, 2 * KEYS * PACK], BF16, align_bytes=64)
+        wb_codes = keep.tile([P, 2 * KEYS], U32, align_bytes=64)
+        wb_scales = keep.tile([P, 2 * KEYS], U8, align_bytes=64)
+
+        def prepare_wkv_b():
+            words = wb_rows[:].bitcast(F32).rearrange("p r (q u) -> p r u q", u=2)
+            turned = ps_turn.tile([P, 2, 2, P], F32, tag="turned")
+            for r in range(2):
+                for u in range(2):
+                    nc.tensor.transpose(turned[:, r, u, :], words[:, r, u, :], ident[:])
+            by_kind = turned[:].rearrange("p r u (g s f) -> p r s g f u", s=2, f=HEAD_KEYS)
+            out_words = wb_grouped[:].bitcast(F32).rearrange(
+                "p (s h f u) -> p s h f u", s=2, h=HEADS, u=2
+            )
+            for r in range(2):
+                for s in range(2):
+                    nc.scalar.copy(out=out_words[:, s, 2 * r : 2 * r + 2, :, :], in_=by_kind[:, r, s])
+            quantise(wb_grouped, wb_codes, wb_scales)
+
+        x_grouped, x_codes, x_scales = {}, {}, {}
+        c_grouped, c_codes, c_scales = {}, {}, {}
+        kv_banks = {}
+        keys_sb, block_max, factors = {}, {}, {}
+
+        def turn_x(n):
+            grouped = stage.tile([P, BLOCK * PACK], BF16, align_bytes=64, tag="x_grouped")
+            turn(x_blocks[n], grouped, nc.vector.tensor_copy)
+            x_grouped[n] = grouped
+
+        def quantise_x(n):
+            codes = stage.tile([P, BLOCK], U32, align_bytes=64, tag="x_codes")
+            scales = stage.tile([P, BLOCK], U8, align_bytes=64, tag="x_scales")
+            quantise(x_grouped[n], codes, scales)
+            x_codes[n], x_scales[n] = codes, scales
+
+        def compress(n):
+            grouped = stage.tile([P, BLOCK * PACK], BF16, align_bytes=64, tag="c_grouped")
+            by_tile = grouped[:].rearrange("p (t r j) -> p t r j", t=TILES, j=PACK)
+            for t in range(TILES):
+                cols = slice(t * P, (t + 1) * P)
+                bank = ps_kvc.tile([P, PACK, P], F32, tag="kvc")
+                for j in range(PACK):
+                    w_cols = slice(j * P, (j + 1) * P)
+                    nc.tensor.matmul_mx(
+                        out=bank[:, j, :],
+                        lhsT=wc_codes[:, w_cols].bitcast(FP8X4),
+                        lhsT_scale=wc_scales[:, w_cols],
+                        rhs=x_codes[n][:, cols].bitcast(FP8X4),
+                        rhs_scale=x_scales[n][:, cols],
+                        start=True,
+                        stop=True,
+                    )
+                nc.scalar.copy(out=by_tile[:, t, :, :], in_=bank[:].rearrange("p j r -> p r j"))
+            c_grouped[n] = grouped
+
+        def quantise_c(n):
+            codes = stage.tile([P, BLOCK], U32, align_bytes=64, tag="c_codes")
+            scales = stage.tile([P, BLOCK], U8, align_bytes=64, tag="c_scales")
+            quantise(c_grouped[n], codes, scales)
+            c_codes[n], c_scales[n] = codes, scales
+
+        def expand(n):
+            raw_keys = ps_kv.tile([P, TILES, KEYS], F32, tag="raw_keys")
+            values = ps_kv.tile([P, TILES, KEYS], F32, tag="values")
+            for s, bank in enumerate((raw_keys, values)):
+                w_cols = slice(s * KEYS, (s + 1) * KEYS)
+                for t in range(TILES):
+                    cols = slice(t * P, (t + 1) * P)
+                    nc.tensor.matmul_mx(
+                        out=bank[:, t, :],
+                        lhsT=c_codes[n][:, cols].bitcast(FP8X4),
+                        lhsT_scale=c_scales[n][:, cols],
+                        rhs=wb_codes[:, w_cols].bitcast(FP8X4),
+                        rhs_scale=wb_scales[:, w_cols],
+                        start=True,
+                        stop=True,
+                    )
+            kv_banks[n] = (raw_keys, values)
+
+        def leave(n):
+            b, rows = rows_of(n)
+            raw_keys, values = kv_banks[n]
+            if n % BLOCKS_PER_BATCH == 0:
+                batch_keys = key_pool.tile([P, ROWS, KEYS], F32)
+                keys_sb[b] = batch_keys
+                maxima = small.tile([P, BLOCKS_PER_BATCH], F32)
+                block_max[b] = maxima
+            nc.scalar.activation(out=keys_sb[b][:, rows, :], in_=raw_keys[:], func=ACT.Silu)
+            v_sb = val_pool.tile([P, TILES, KEYS], F32)
+            nc.scalar.copy(out=v_sb[:], in_=values[:])
+            nc.sync.dma_start(out=v_rows[b, :, rows, :], in_=v_sb[:])
+
+        def maximum(n):
+            b, rows = rows_of(n)
+            place = n % BLOCKS_PER_BATCH
+            nc.vector.tensor_reduce(
+                out=block_max[b][:, place : place + 1],
+                in_=keys_sb[b][:, rows, :].rearrange("p i f -> p (i f)"),
+                axis=AXIS.X,
+                op=ALU.max,
+            )
+
+        repeated = {}
+
+        def repeat_maxima(b):
+            own = small.tile([P, 1], F32)
+            nc.vector.tensor_reduce(out=own[:], in_=block_max[b][:], axis=AXIS.X, op=ALU.max)
+            rep = small.tile([P, P], F32)
+            nc.vector.tensor_copy(out=rep[:], in_=own[:].to_broadcast([P, P]))
+            repeated[b] = rep
+
+        def make_factors(b):
+            spread = ps_kvc.tile([P, P], F32, tag="kvc")
+            nc.tensor.transpose(spread[:], repeated[b][:], ident[:])
+            group_max = small.tile([P, HEADS], F32)
+            nc.vector.tensor_reduce(
+                out=group_max[:],
+                in_=spread[:].rearrange("p (g q) -> p g q", g=HEADS),
+                axis=AXIS.X,
+                op=ALU.max,
+            )
+            divisor = small.tile([P, HEADS], F32)
+            nc.vector.scalar_tensor_tensor(
+                out=divisor[:], in0=group_max[:], scalar=0.0, in1=group_max[:],
+                op0=ALU.is_equal, op1=ALU.add,
+            )
+            inverse = small.tile([P, HEADS], F32)
+            nc.vector.reciprocal(out=inverse[:], in_=divisor[:])
+            eta = small.tile([P, HEADS], F32)
+            nc.vector.tensor_scalar(
+                out=eta[:], in0=inverse[:], scalar1=10.0, scalar2=1.0, op0=ALU.mult, op1=ALU.min
+            )
+            factors[b] = eta
+
+        def scale_head(b, h):
+            head = keys_sb[b][:, :, h * HEAD_KEYS : (h + 1) * HEAD_KEYS]
+            nc.vector.tensor_scalar(
+                out=head, in0=head, scalar1=factors[b][:, h : h + 1], scalar2=None, op0=ALU.mult
+            )
+
+        def live(n):
+            return 0 <= n < N_BLOCKS
+
+        for t in range(N_BLOCKS + 7):
+            if live(t - 2):
+                quantise_c(t - 2)
+            if live(t - 3):
+                leave(t - 3)
+            late = t - 7
+            if live(late) and late % HEADS == 0:
+                make_factors(late // HEADS)
+            if t == 1:
+                prepare_wkv_b()
+            if live(t):
+                turn_x(t)
+            if live(t - 1):
+                compress(t - 1)
+            if live(t - 2):
+                expand(t - 2)
+            if live(t - 3):
+                maximum(t - 3)
+                if (t - 3) % BLOCKS_PER_BATCH == BLOCKS_PER_BATCH - 1:
+                    repeat_maxima((t - 3) // BLOCKS_PER_BATCH)
+            if live(t):
+                quantise_x(t)
+            if live(late):
+                scale_head(late // HEADS, late % HEADS)
+                if late % HEADS == HEADS - 1:
+                    nc.sync.dma_start(out=k_rows[late // HEADS], in_=keys_sb[late // HEADS][:])

@@ -22,6 +22,7 @@ TILES = 4
 BLOCK = TILES * P
 BLOCKS_PER_BATCH = ROWS // TILES
 N_BLOCKS = BATCHES * BLOCKS_PER_BATCH
+VECTOR_VALUES_EVERY = 4
 
 FLOPS = 2 * BATCHES * SEQ * D * (D + 2 * KEYS)
 
@@ -57,7 +58,7 @@ def tile_ssa_pb_t_kernel(tc, x, wkv_c, wkv_b, out_0, out_1):
             x_block = x_pool.tile([P, TILES, D], BF16)
             nc.sync.dma_start(out=x_block[:], in_=x_rows[b, :, rows, :])
             x_blocks[n] = x_block
-            if n == 0:
+            if n == 1:
                 nc.sync.dma_start(out=wb_rows[:], in_=wkv_b.rearrange("(r p) c -> p r c", p=P))
 
         ident = keep.tile([P, P], F32)
@@ -68,19 +69,25 @@ def tile_ssa_pb_t_kernel(tc, x, wkv_c, wkv_b, out_0, out_1):
         warm = keep.tile([P, 1], F32)
         nc.scalar.activation(out=warm[:], in_=zero[:], func=ACT.Silu)
 
-        def turn(rows_sb, grouped, copy):
+        def turn(rows_sb, pool, tag):
             words = rows_sb[:].bitcast(F32)
-            out_words = grouped[:].bitcast(F32).rearrange("p (t r u) -> p t r u", t=TILES, u=2)
+            banks = []
             for half in range(2):
-                turned = ps_turn.tile([P, 2, 2, P], F32, tag="turned")
+                turned = pool.tile([P, 2, 2, P], F32, tag=tag)
                 for t in range(2):
                     for u in range(2):
                         nc.tensor.transpose(
                             turned[:, t, u, :], words[:, 2 * half + t, u * P : (u + 1) * P], ident[:]
                         )
-                copy(
+                banks.append(turned)
+            return banks
+
+        def regroup(banks, grouped, copies):
+            out_words = grouped[:].bitcast(F32).rearrange("p (t r u) -> p t r u", t=TILES, u=2)
+            for half in range(2):
+                copies[half](
                     out=out_words[:, 2 * half : 2 * half + 2, :, :],
-                    in_=turned[:].rearrange("p t u r -> p t r u"),
+                    in_=banks[half][:].rearrange("p t u r -> p t r u"),
                 )
 
         def quantise(grouped, codes, scales):
@@ -89,16 +96,13 @@ def tile_ssa_pb_t_kernel(tc, x, wkv_c, wkv_b, out_0, out_1):
         wc_grouped = keep.tile([P, BLOCK * PACK], BF16, align_bytes=64)
         wc_codes = keep.tile([P, BLOCK], U32, align_bytes=64)
         wc_scales = keep.tile([P, BLOCK], U8, align_bytes=64)
-        turn(wc_rows, wc_grouped, nc.scalar.copy)
-        quantise(wc_grouped, wc_codes, wc_scales)
-
         wb_grouped = keep.tile([P, 2 * KEYS * PACK], BF16, align_bytes=64)
         wb_codes = keep.tile([P, 2 * KEYS], U32, align_bytes=64)
         wb_scales = keep.tile([P, 2 * KEYS], U8, align_bytes=64)
 
-        def prepare_wkv_b():
+        def turn_wkv_b():
             words = wb_rows[:].bitcast(F32).rearrange("p r (q u) -> p r u q", u=2)
-            turned = ps_turn.tile([P, 2, 2, P], F32, tag="turned")
+            turned = ps_kv.tile([P, 2, 2, P], F32, tag="values")
             for r in range(2):
                 for u in range(2):
                     nc.tensor.transpose(turned[:, r, u, :], words[:, r, u, :], ident[:])
@@ -109,16 +113,19 @@ def tile_ssa_pb_t_kernel(tc, x, wkv_c, wkv_b, out_0, out_1):
             for r in range(2):
                 for s in range(2):
                     nc.scalar.copy(out=out_words[:, s, 2 * r : 2 * r + 2, :, :], in_=by_kind[:, r, s])
-            quantise(wb_grouped, wb_codes, wb_scales)
 
-        x_grouped, x_codes, x_scales = {}, {}, {}
+        x_turned, x_grouped, x_codes, x_scales = {}, {}, {}, {}
         c_grouped, c_codes, c_scales = {}, {}, {}
-        kv_banks = {}
+        key_banks, value_banks = {}, {}
         keys_sb, block_max, factors = {}, {}, {}
 
         def turn_x(n):
+            x_turned[n] = turn(x_blocks[n], ps_turn, "turned")
+
+        def regroup_x(n):
             grouped = stage.tile([P, BLOCK * PACK], BF16, align_bytes=64, tag="x_grouped")
-            turn(x_blocks[n], grouped, nc.vector.tensor_copy)
+            first = nc.scalar.copy if n == 0 else nc.vector.tensor_copy
+            regroup(x_turned[n], grouped, (first, nc.vector.tensor_copy))
             x_grouped[n] = grouped
 
         def quantise_x(n):
@@ -144,7 +151,9 @@ def tile_ssa_pb_t_kernel(tc, x, wkv_c, wkv_b, out_0, out_1):
                         start=True,
                         stop=True,
                     )
-                nc.scalar.copy(out=by_tile[:, t, :, :], in_=bank[:].rearrange("p j r -> p r j"))
+                shared = n == N_BLOCKS - 1 and t >= TILES // 2
+                copy = nc.vector.tensor_copy if shared else nc.scalar.copy
+                copy(out=by_tile[:, t, :, :], in_=bank[:].rearrange("p j r -> p r j"))
             c_grouped[n] = grouped
 
         def quantise_c(n):
@@ -153,35 +162,45 @@ def tile_ssa_pb_t_kernel(tc, x, wkv_c, wkv_b, out_0, out_1):
             quantise(c_grouped[n], codes, scales)
             c_codes[n], c_scales[n] = codes, scales
 
-        def expand(n):
-            raw_keys = ps_kv.tile([P, TILES, KEYS], F32, tag="raw_keys")
-            values = ps_kv.tile([P, TILES, KEYS], F32, tag="values")
-            for s, bank in enumerate((raw_keys, values)):
-                w_cols = slice(s * KEYS, (s + 1) * KEYS)
-                for t in range(TILES):
-                    cols = slice(t * P, (t + 1) * P)
-                    nc.tensor.matmul_mx(
-                        out=bank[:, t, :],
-                        lhsT=c_codes[n][:, cols].bitcast(FP8X4),
-                        lhsT_scale=c_scales[n][:, cols],
-                        rhs=wb_codes[:, w_cols].bitcast(FP8X4),
-                        rhs_scale=wb_scales[:, w_cols],
-                        start=True,
-                        stop=True,
-                    )
-            kv_banks[n] = (raw_keys, values)
+        def expand(n, kind, bank):
+            w_cols = slice(kind * KEYS, (kind + 1) * KEYS)
+            for t in range(TILES):
+                cols = slice(t * P, (t + 1) * P)
+                nc.tensor.matmul_mx(
+                    out=bank[:, t, :],
+                    lhsT=c_codes[n][:, cols].bitcast(FP8X4),
+                    lhsT_scale=c_scales[n][:, cols],
+                    rhs=wb_codes[:, w_cols].bitcast(FP8X4),
+                    rhs_scale=wb_scales[:, w_cols],
+                    start=True,
+                    stop=True,
+                )
 
-        def leave(n):
+        def expand_keys(n):
+            raw_keys = ps_kv.tile([P, TILES, KEYS], F32, tag="raw_keys")
+            expand(n, 0, raw_keys)
+            key_banks[n] = raw_keys
+
+        def expand_values(n):
+            values = ps_kv.tile([P, TILES, KEYS], F32, tag="values")
+            expand(n, 1, values)
+            value_banks[n] = values
+
+        def leave_keys(n):
             b, rows = rows_of(n)
-            raw_keys, values = kv_banks[n]
             if n % BLOCKS_PER_BATCH == 0:
                 batch_keys = key_pool.tile([P, ROWS, KEYS], F32)
                 keys_sb[b] = batch_keys
                 maxima = small.tile([P, BLOCKS_PER_BATCH], F32)
                 block_max[b] = maxima
-            nc.scalar.activation(out=keys_sb[b][:, rows, :], in_=raw_keys[:], func=ACT.Silu)
+            nc.scalar.activation(out=keys_sb[b][:, rows, :], in_=key_banks[n][:], func=ACT.Silu)
+
+        def leave_values(n):
+            b, rows = rows_of(n)
             v_sb = val_pool.tile([P, TILES, KEYS], F32)
-            nc.scalar.copy(out=v_sb[:], in_=values[:])
+            to_vector = n % VECTOR_VALUES_EVERY == VECTOR_VALUES_EVERY // 2
+            copy = nc.vector.tensor_copy if to_vector else nc.scalar.copy
+            copy(out=v_sb[:], in_=value_banks[n][:])
             nc.sync.dma_start(out=v_rows[b, :, rows, :], in_=v_sb[:])
 
         def maximum(n):
@@ -194,7 +213,7 @@ def tile_ssa_pb_t_kernel(tc, x, wkv_c, wkv_b, out_0, out_1):
                 op=ALU.max,
             )
 
-        repeated = {}
+        repeated, spread_banks = {}, {}
 
         def repeat_maxima(b):
             own = small.tile([P, 1], F32)
@@ -203,13 +222,16 @@ def tile_ssa_pb_t_kernel(tc, x, wkv_c, wkv_b, out_0, out_1):
             nc.vector.tensor_copy(out=rep[:], in_=own[:].to_broadcast([P, P]))
             repeated[b] = rep
 
-        def make_factors(b):
-            spread = ps_kvc.tile([P, P], F32, tag="kvc")
+        def spread_maxima(b):
+            spread = ps_kv.tile([P, P], F32, tag="values")
             nc.tensor.transpose(spread[:], repeated[b][:], ident[:])
+            spread_banks[b] = spread
+
+        def make_factors(b):
             group_max = small.tile([P, HEADS], F32)
             nc.vector.tensor_reduce(
                 out=group_max[:],
-                in_=spread[:].rearrange("p (g q) -> p g q", g=HEADS),
+                in_=spread_banks[b][:].rearrange("p (g q) -> p g q", g=HEADS),
                 axis=AXIS.X,
                 op=ALU.max,
             )
@@ -226,38 +248,73 @@ def tile_ssa_pb_t_kernel(tc, x, wkv_c, wkv_b, out_0, out_1):
             )
             factors[b] = eta
 
-        def scale_head(b, h):
-            head = keys_sb[b][:, :, h * HEAD_KEYS : (h + 1) * HEAD_KEYS]
-            nc.vector.tensor_scalar(
-                out=head, in0=head, scalar1=factors[b][:, h : h + 1], scalar2=None, op0=ALU.mult
+        def head_of(b, h):
+            return keys_sb[b][:, :, h * HEAD_KEYS : (h + 1) * HEAD_KEYS], factors[b][:, h : h + 1]
+
+        def scale_on_gpsimd(b, h):
+            head, eta = head_of(b, h)
+            nc.gpsimd.tensor_scalar(
+                out=head, in0=head, scalar1=eta, scalar2=1.0, op0=ALU.mult, op1=ALU.mult
             )
+
+        def scale_on_vector(b, h):
+            head, eta = head_of(b, h)
+            nc.vector.tensor_scalar(out=head, in0=head, scalar1=eta, scalar2=None, op0=ALU.mult)
+
+        def scale_on_scalar(b, h):
+            head, eta = head_of(b, h)
+            nc.scalar.activation(out=head, in_=head, func=ACT.Copy, scale=eta)
+
+        def store_keys(b):
+            nc.sync.dma_start(out=k_rows[b], in_=keys_sb[b][:])
 
         def live(n):
             return 0 <= n < N_BLOCKS
 
-        for t in range(N_BLOCKS + 7):
+        regroup(turn(wc_rows, ps_kvc, "kvc"), wc_grouped, (nc.vector.tensor_copy, nc.scalar.copy))
+        quantise(wc_grouped, wc_codes, wc_scales)
+        turn_x(0)
+
+        for t in range(N_BLOCKS + 4):
+            late = t - 7
+            new_factors = live(late) and late % HEADS == 0
+            if live(t):
+                regroup_x(t)
             if live(t - 2):
                 quantise_c(t - 2)
             if live(t - 3):
-                leave(t - 3)
-            late = t - 7
-            if live(late) and late % HEADS == 0:
-                make_factors(late // HEADS)
-            if t == 1:
-                prepare_wkv_b()
-            if live(t):
-                turn_x(t)
+                leave_keys(t - 3)
+                leave_values(t - 3)
             if live(t - 1):
                 compress(t - 1)
+            if new_factors:
+                spread_maxima(late // HEADS)
+            if live(t + 1):
+                turn_x(t + 1)
+            if t == 0:
+                turn_wkv_b()
             if live(t - 2):
-                expand(t - 2)
+                expand_keys(t - 2)
+            if live(t):
+                quantise_x(t)
+            if t == 1:
+                quantise(wb_grouped, wb_codes, wb_scales)
+            if new_factors:
+                make_factors(late // HEADS)
+            if live(t - 2):
+                expand_values(t - 2)
             if live(t - 3):
                 maximum(t - 3)
                 if (t - 3) % BLOCKS_PER_BATCH == BLOCKS_PER_BATCH - 1:
                     repeat_maxima((t - 3) // BLOCKS_PER_BATCH)
-            if live(t):
-                quantise_x(t)
-            if live(late):
-                scale_head(late // HEADS, late % HEADS)
+            if live(late) and late // HEADS < BATCHES - 1:
+                scale_on_gpsimd(late // HEADS, late % HEADS)
                 if late % HEADS == HEADS - 1:
-                    nc.sync.dma_start(out=k_rows[late // HEADS], in_=keys_sb[late // HEADS][:])
+                    store_keys(late // HEADS)
+
+        last = BATCHES - 1
+        scale_on_vector(last, 0)
+        scale_on_scalar(last, 2)
+        scale_on_gpsimd(last, 3)
+        scale_on_vector(last, 1)
+        store_keys(last)

@@ -39,7 +39,6 @@ def tile_ssa_pb_t_kernel(tc, x, wkv_c, wkv_b, out_0, out_1):
         ps_turn = ctx.enter_context(tc.psum_pool(name="ps_turn", bufs=2))
         ps_kvc = ctx.enter_context(tc.psum_pool(name="ps_kvc", bufs=4))
         ps_kv = ctx.enter_context(tc.psum_pool(name="ps_kv", bufs=1))
-        ctx.enter_context(tc.manual_schedule())
 
         x_rows = x.rearrange("b (p i) d -> b p i d", i=ROWS)
         k_rows = out_0.rearrange("b (p i) h f -> b p i (h f)", i=ROWS)

@@ -22,6 +22,7 @@ TILES = 4
 BLOCK = TILES * P
 BLOCKS_PER_BATCH = ROWS // TILES
 N_BLOCKS = BATCHES * BLOCKS_PER_BATCH
+HALVES = (slice(0, TILES // 2), slice(TILES // 2, TILES))
 VECTOR_VALUES_EVERY = 4
 
 FLOPS = 2 * BATCHES * SEQ * D * (D + 2 * KEYS)
@@ -49,13 +50,17 @@ def tile_ssa_pb_t_kernel(tc, x, wkv_c, wkv_b, out_0, out_1):
             return n // BLOCKS_PER_BATCH, slice(first, first + TILES)
 
         wc_rows = keep.tile([P, TILES, D], BF16)
-        nc.sync.dma_start(out=wc_rows[:], in_=wkv_c.rearrange("(m j) d -> m j d", j=PACK))
+        wc_halves = wkv_c.rearrange("(m j) d -> m j d", j=PACK)
+        for half in HALVES:
+            nc.sync.dma_start(out=wc_rows[:, half, :], in_=wc_halves[:, half, :])
         wb_rows = keep.tile([P, 2, D], BF16)
         x_blocks = {}
         for n in range(N_BLOCKS):
             b, rows = rows_of(n)
             x_block = x_pool.tile([P, TILES, D], BF16)
-            nc.sync.dma_start(out=x_block[:], in_=x_rows[b, :, rows, :])
+            for part in HALVES if n == 0 else (slice(0, TILES),):
+                some = slice(rows.start + part.start, rows.start + part.stop)
+                nc.sync.dma_start(out=x_block[:, part, :], in_=x_rows[b, :, some, :])
             x_blocks[n] = x_block
             if n == 1:
                 nc.sync.dma_start(out=wb_rows[:], in_=wkv_b.rearrange("(r p) c -> p r c", p=P))
@@ -91,6 +96,15 @@ def tile_ssa_pb_t_kernel(tc, x, wkv_c, wkv_b, out_0, out_1):
 
         def quantise(grouped, codes, scales):
             nc.vector.quantize_mx(out=codes[:].bitcast(FP8X4), scales=scales[:], in_=grouped[:])
+
+        def quantise_halves(grouped, codes, scales):
+            for half in HALVES:
+                cols = slice(half.start * P, half.stop * P)
+                nc.vector.quantize_mx(
+                    out=codes[:, cols].bitcast(FP8X4),
+                    scales=scales[:, cols],
+                    in_=grouped[:, cols.start * PACK : cols.stop * PACK],
+                )
 
         wc_grouped = keep.tile([P, BLOCK * PACK], BF16, align_bytes=64)
         wc_codes = keep.tile([P, BLOCK], U32, align_bytes=64)
@@ -130,7 +144,7 @@ def tile_ssa_pb_t_kernel(tc, x, wkv_c, wkv_b, out_0, out_1):
         def quantise_x(n):
             codes = stage.tile([P, BLOCK], U32, align_bytes=64, tag="x_codes")
             scales = stage.tile([P, BLOCK], U8, align_bytes=64, tag="x_scales")
-            quantise(x_grouped[n], codes, scales)
+            (quantise_halves if n == 0 else quantise)(x_grouped[n], codes, scales)
             x_codes[n], x_scales[n] = codes, scales
 
         def compress(n):
@@ -212,18 +226,16 @@ def tile_ssa_pb_t_kernel(tc, x, wkv_c, wkv_b, out_0, out_1):
                 op=ALU.max,
             )
 
-        repeated, spread_banks = {}, {}
+        own_max, spread_banks = {}, {}
 
-        def repeat_maxima(b):
+        def join_maxima(b):
             own = small.tile([P, 1], F32)
             nc.vector.tensor_reduce(out=own[:], in_=block_max[b][:], axis=AXIS.X, op=ALU.max)
-            rep = small.tile([P, P], F32)
-            nc.vector.tensor_copy(out=rep[:], in_=own[:].to_broadcast([P, P]))
-            repeated[b] = rep
+            own_max[b] = own
 
         def spread_maxima(b):
             spread = ps_kv.tile([P, P], F32, tag="values")
-            nc.tensor.transpose(spread[:], repeated[b][:], ident[:])
+            nc.tensor.transpose(spread[:], own_max[b][:].to_broadcast([P, P]), ident[:])
             spread_banks[b] = spread
 
         def make_factors(b):
@@ -271,7 +283,7 @@ def tile_ssa_pb_t_kernel(tc, x, wkv_c, wkv_b, out_0, out_1):
             return 0 <= n < N_BLOCKS
 
         regroup(turn(wc_rows, ps_kvc, "kvc"), wc_grouped, (nc.vector.tensor_copy, nc.scalar.copy))
-        quantise(wc_grouped, wc_codes, wc_scales)
+        quantise_halves(wc_grouped, wc_codes, wc_scales)
         turn_x(0)
 
         for t in range(N_BLOCKS + 4):
@@ -305,7 +317,7 @@ def tile_ssa_pb_t_kernel(tc, x, wkv_c, wkv_b, out_0, out_1):
             if live(t - 3):
                 maximum(t - 3)
                 if (t - 3) % BLOCKS_PER_BATCH == BLOCKS_PER_BATCH - 1:
-                    repeat_maxima((t - 3) // BLOCKS_PER_BATCH)
+                    join_maxima((t - 3) // BLOCKS_PER_BATCH)
             if live(late) and late // HEADS < BATCHES - 1:
                 scale_on_gpsimd(late // HEADS, late % HEADS)
                 if late % HEADS == HEADS - 1:

@@ -35,11 +35,11 @@ def tile_ssa_pb_t_kernel(tc, x, wkv_c, wkv_b, out_0, out_1):
         x_pool = ctx.enter_context(tc.tile_pool(name="x_pool", bufs=N_BLOCKS))
         stage = ctx.enter_context(tc.tile_pool(name="stage", bufs=2))
         key_pool = ctx.enter_context(tc.tile_pool(name="key_pool", bufs=BATCHES))
-        val_pool = ctx.enter_context(tc.tile_pool(name="val_pool", bufs=4))
+        val_pool = ctx.enter_context(tc.tile_pool(name="val_pool", bufs=N_BLOCKS))
         small = ctx.enter_context(tc.tile_pool(name="small", bufs=BATCHES))
         ps_turn = ctx.enter_context(tc.psum_pool(name="ps_turn", bufs=2))
         ps_kvc = ctx.enter_context(tc.psum_pool(name="ps_kvc", bufs=4))
-        ps_kv = ctx.enter_context(tc.psum_pool(name="ps_kv", bufs=1))
+        ps_kv = ctx.enter_context(tc.psum_pool(name="ps_kv", bufs=2))
 
         x_rows = x.rearrange("b (p i) d -> b p i d", i=ROWS)
         k_rows = out_0.rearrange("b (p i) h f -> b p i (h f)", i=ROWS)
@@ -62,7 +62,7 @@ def tile_ssa_pb_t_kernel(tc, x, wkv_c, wkv_b, out_0, out_1):
                 some = slice(rows.start + part.start, rows.start + part.stop)
                 nc.sync.dma_start(out=x_block[:, part, :], in_=x_rows[b, :, some, :])
             x_blocks[n] = x_block
-            if n == 1:
+            if n == 0:
                 nc.sync.dma_start(out=wb_rows[:], in_=wkv_b.rearrange("(r p) c -> p r c", p=P))
 
         ident = keep.tile([P, P], F32)
@@ -88,7 +88,7 @@ def tile_ssa_pb_t_kernel(tc, x, wkv_c, wkv_b, out_0, out_1):
 
         def regroup(banks, grouped, copies):
             out_words = grouped[:].bitcast(F32).rearrange("p (t r u) -> p t r u", t=TILES, u=2)
-            for half in range(2):
+            for half in (1, 0):
                 copies[half](
                     out=out_words[:, 2 * half : 2 * half + 2, :, :],
                     in_=banks[half][:].rearrange("p t u r -> p t r u"),
@@ -115,7 +115,7 @@ def tile_ssa_pb_t_kernel(tc, x, wkv_c, wkv_b, out_0, out_1):
 
         def turn_wkv_b():
             words = wb_rows[:].bitcast(F32).rearrange("p r (q u) -> p r u q", u=2)
-            turned = ps_kv.tile([P, 2, 2, P], F32, tag="values")
+            turned = ps_kv.tile([P, 2, 2, P], F32, tag="kv")
             for r in range(2):
                 for u in range(2):
                     nc.tensor.transpose(turned[:, r, u, :], words[:, r, u, :], ident[:])
@@ -129,7 +129,7 @@ def tile_ssa_pb_t_kernel(tc, x, wkv_c, wkv_b, out_0, out_1):
 
         x_turned, x_grouped, x_codes, x_scales = {}, {}, {}, {}
         c_grouped, c_codes, c_scales = {}, {}, {}
-        key_banks, value_banks = {}, {}
+        kv_banks = {}
         keys_sb, block_max, factors = {}, {}, {}
 
         def turn_x(n):
@@ -164,7 +164,7 @@ def tile_ssa_pb_t_kernel(tc, x, wkv_c, wkv_b, out_0, out_1):
                         start=True,
                         stop=True,
                     )
-                shared = n == N_BLOCKS - 1 and t >= TILES // 2
+                shared = n == N_BLOCKS - 1 and t % 2 == 1
                 copy = nc.vector.tensor_copy if shared else nc.scalar.copy
                 copy(out=by_tile[:, t, :, :], in_=bank[:].rearrange("p j r -> p r j"))
             c_grouped[n] = grouped
@@ -172,32 +172,26 @@ def tile_ssa_pb_t_kernel(tc, x, wkv_c, wkv_b, out_0, out_1):
         def quantise_c(n):
             codes = stage.tile([P, BLOCK], U32, align_bytes=64, tag="c_codes")
             scales = stage.tile([P, BLOCK], U8, align_bytes=64, tag="c_scales")
-            quantise(c_grouped[n], codes, scales)
+            (quantise_halves if n == N_BLOCKS - 1 else quantise)(c_grouped[n], codes, scales)
             c_codes[n], c_scales[n] = codes, scales
 
-        def expand(n, kind, bank):
-            w_cols = slice(kind * KEYS, (kind + 1) * KEYS)
-            for t in range(TILES):
-                cols = slice(t * P, (t + 1) * P)
-                nc.tensor.matmul_mx(
-                    out=bank[:, t, :],
-                    lhsT=c_codes[n][:, cols].bitcast(FP8X4),
-                    lhsT_scale=c_scales[n][:, cols],
-                    rhs=wb_codes[:, w_cols].bitcast(FP8X4),
-                    rhs_scale=wb_scales[:, w_cols],
-                    start=True,
-                    stop=True,
-                )
-
-        def expand_keys(n):
-            raw_keys = ps_kv.tile([P, TILES, KEYS], F32, tag="raw_keys")
-            expand(n, 0, raw_keys)
-            key_banks[n] = raw_keys
-
-        def expand_values(n):
-            values = ps_kv.tile([P, TILES, KEYS], F32, tag="values")
-            expand(n, 1, values)
-            value_banks[n] = values
+        def expand(n):
+            kv_banks[n] = []
+            for half in HALVES:
+                pool, tag = (ps_kvc, "kvc") if n == N_BLOCKS - 1 else (ps_kv, "kv")
+                bank = pool.tile([P, TILES // 2, 2, KEYS], F32, tag=tag)
+                for t in range(half.start, half.stop):
+                    cols = slice(t * P, (t + 1) * P)
+                    nc.tensor.matmul_mx(
+                        out=bank[:, t - half.start].rearrange("p s f -> p (s f)"),
+                        lhsT=c_codes[n][:, cols].bitcast(FP8X4),
+                        lhsT_scale=c_scales[n][:, cols],
+                        rhs=wb_codes[:].bitcast(FP8X4),
+                        rhs_scale=wb_scales[:],
+                        start=True,
+                        stop=True,
+                    )
+                kv_banks[n].append(bank)
 
         def leave_keys(n):
             b, rows = rows_of(n)
@@ -206,14 +200,19 @@ def tile_ssa_pb_t_kernel(tc, x, wkv_c, wkv_b, out_0, out_1):
                 keys_sb[b] = batch_keys
                 maxima = small.tile([P, BLOCKS_PER_BATCH], F32)
                 block_max[b] = maxima
-            nc.scalar.activation(out=keys_sb[b][:, rows, :], in_=key_banks[n][:], func=ACT.Silu)
+            for bank, half in zip(kv_banks[n], HALVES):
+                some = slice(rows.start + half.start, rows.start + half.stop)
+                nc.scalar.activation(
+                    out=keys_sb[b][:, some, :], in_=bank[:, :, 0, :], func=ACT.Silu
+                )
 
         def leave_values(n):
             b, rows = rows_of(n)
             v_sb = val_pool.tile([P, TILES, KEYS], F32)
             to_vector = n % VECTOR_VALUES_EVERY == VECTOR_VALUES_EVERY // 2
             copy = nc.vector.tensor_copy if to_vector else nc.scalar.copy
-            copy(out=v_sb[:], in_=value_banks[n][:])
+            for bank, half in zip(kv_banks[n], HALVES):
+                copy(out=v_sb[:, half, :], in_=bank[:, :, 1, :])
             nc.sync.dma_start(out=v_rows[b, :, rows, :], in_=v_sb[:])
 
         def maximum(n):
@@ -234,7 +233,7 @@ def tile_ssa_pb_t_kernel(tc, x, wkv_c, wkv_b, out_0, out_1):
             own_max[b] = own
 
         def spread_maxima(b):
-            spread = ps_kv.tile([P, P], F32, tag="values")
+            spread = ps_kv.tile([P, P], F32, tag="kv")
             nc.tensor.transpose(spread[:], own_max[b][:].to_broadcast([P, P]), ident[:])
             spread_banks[b] = spread
 
@@ -305,15 +304,13 @@ def tile_ssa_pb_t_kernel(tc, x, wkv_c, wkv_b, out_0, out_1):
             if t == 0:
                 turn_wkv_b()
             if live(t - 2):
-                expand_keys(t - 2)
+                expand(t - 2)
             if live(t):
                 quantise_x(t)
             if t == 1:
                 quantise(wb_grouped, wb_codes, wb_scales)
             if new_factors:
                 make_factors(late // HEADS)
-            if live(t - 2):
-                expand_values(t - 2)
             if live(t - 3):
                 maximum(t - 3)
                 if (t - 3) % BLOCKS_PER_BATCH == BLOCKS_PER_BATCH - 1:

from contextlib import ExitStack

import concourse.mybir as mybir
from concourse.masks import make_identity

F32 = mybir.dt.float32
BF16 = mybir.dt.bfloat16
U32 = mybir.dt.uint32
U8 = mybir.dt.uint8
FP8X4 = mybir.dt.float8_e4m3fn_x4
ACT = mybir.ActivationFunctionType
ALU = mybir.AluOpType
AXIS = mybir.AxisListType

P = 128
PACK = 4
BATCHES, SEQ, D = 4, 2048, 512
HEADS, HEAD_KEYS = 4, 32
KEYS = HEADS * HEAD_KEYS
ROWS = SEQ // P
TILES = 4
BLOCK = TILES * P
BLOCKS_PER_BATCH = ROWS // TILES
N_BLOCKS = BATCHES * BLOCKS_PER_BATCH
HALVES = (slice(0, TILES // 2), slice(TILES // 2, TILES))
VECTOR_VALUES_EVERY = 4

FLOPS = 2 * BATCHES * SEQ * D * (D + 2 * KEYS)


def tile_ssa_pb_t_kernel(tc, x, wkv_c, wkv_b, out_0, out_1):
    nc = tc.nc
    with ExitStack() as ctx:
        keep = ctx.enter_context(tc.tile_pool(name="keep", bufs=1))
        x_pool = ctx.enter_context(tc.tile_pool(name="x_pool", bufs=N_BLOCKS))
        stage = ctx.enter_context(tc.tile_pool(name="stage", bufs=2))
        key_pool = ctx.enter_context(tc.tile_pool(name="key_pool", bufs=BATCHES))
        val_pool = ctx.enter_context(tc.tile_pool(name="val_pool", bufs=N_BLOCKS))
        small = ctx.enter_context(tc.tile_pool(name="small", bufs=BATCHES))
        ps_turn = ctx.enter_context(tc.psum_pool(name="ps_turn", bufs=2))
        ps_kvc = ctx.enter_context(tc.psum_pool(name="ps_kvc", bufs=4))
        ps_kv = ctx.enter_context(tc.psum_pool(name="ps_kv", bufs=2))

        x_rows = x.rearrange("b (p i) d -> b p i d", i=ROWS)
        k_rows = out_0.rearrange("b (p i) h f -> b p i (h f)", i=ROWS)
        v_rows = out_1.rearrange("b (p i) h f -> b p i (h f)", i=ROWS)

        def rows_of(n):
            first = (n % BLOCKS_PER_BATCH) * TILES
            return n // BLOCKS_PER_BATCH, slice(first, first + TILES)

        wc_rows = keep.tile([P, TILES, D], BF16)
        wc_halves = wkv_c.rearrange("(m j) d -> m j d", j=PACK)
        for half in HALVES:
            nc.sync.dma_start(out=wc_rows[:, half, :], in_=wc_halves[:, half, :])
        wb_rows = keep.tile([P, 2, D], BF16)
        x_blocks = {}
        for n in range(N_BLOCKS):
            b, rows = rows_of(n)
            x_block = x_pool.tile([P, TILES, D], BF16)
            for part in HALVES if n == 0 else (slice(0, TILES),):
                some = slice(rows.start + part.start, rows.start + part.stop)
                nc.sync.dma_start(out=x_block[:, part, :], in_=x_rows[b, :, some, :])
            x_blocks[n] = x_block
            if n == 0:
                nc.sync.dma_start(out=wb_rows[:], in_=wkv_b.rearrange("(r p) c -> p r c", p=P))

        ident = keep.tile([P, P], F32)
        make_identity(nc, ident[:])

        zero = keep.tile([P, 1], F32)
        nc.vector.memset(zero[:], 0.0)
        warm = keep.tile([P, 1], F32)
        nc.scalar.activation(out=warm[:], in_=zero[:], func=ACT.Silu)

        def turn(rows_sb, pool, tag):
            words = rows_sb[:].bitcast(F32)
            banks = []
            for half in range(2):
                turned = pool.tile([P, 2, 2, P], F32, tag=tag)
                for t in range(2):
                    for u in range(2):
                        nc.tensor.transpose(
                            turned[:, t, u, :], words[:, 2 * half + t, u * P : (u + 1) * P], ident[:]
                        )
                banks.append(turned)
            return banks

        def regroup(banks, grouped, copies):
            out_words = grouped[:].bitcast(F32).rearrange("p (t r u) -> p t r u", t=TILES, u=2)
            for half in (1, 0):
                copies[half](
                    out=out_words[:, 2 * half : 2 * half + 2, :, :],
                    in_=banks[half][:].rearrange("p t u r -> p t r u"),
                )

        def quantise(grouped, codes, scales):
            nc.vector.quantize_mx(out=codes[:].bitcast(FP8X4), scales=scales[:], in_=grouped[:])

        def quantise_halves(grouped, codes, scales):
            for half in HALVES:
                cols = slice(half.start * P, half.stop * P)
                nc.vector.quantize_mx(
                    out=codes[:, cols].bitcast(FP8X4),
                    scales=scales[:, cols],
                    in_=grouped[:, cols.start * PACK : cols.stop * PACK],
                )

        wc_grouped = keep.tile([P, BLOCK * PACK], BF16, align_bytes=64)
        wc_codes = keep.tile([P, BLOCK], U32, align_bytes=64)
        wc_scales = keep.tile([P, BLOCK], U8, align_bytes=64)
        wb_grouped = keep.tile([P, 2 * KEYS * PACK], BF16, align_bytes=64)
        wb_codes = keep.tile([P, 2 * KEYS], U32, align_bytes=64)
        wb_scales = keep.tile([P, 2 * KEYS], U8, align_bytes=64)

        def turn_wkv_b():
            words = wb_rows[:].bitcast(F32).rearrange("p r (q u) -> p r u q", u=2)
            turned = ps_kv.tile([P, 2, 2, P], F32, tag="kv")
            for r in range(2):
                for u in range(2):
                    nc.tensor.transpose(turned[:, r, u, :], words[:, r, u, :], ident[:])
            by_kind = turned[:].rearrange("p r u (g s f) -> p r s g f u", s=2, f=HEAD_KEYS)
            out_words = wb_grouped[:].bitcast(F32).rearrange(
                "p (s h f u) -> p s h f u", s=2, h=HEADS, u=2
            )
            for r in range(2):
                for s in range(2):
                    nc.scalar.copy(out=out_words[:, s, 2 * r : 2 * r + 2, :, :], in_=by_kind[:, r, s])

        x_turned, x_grouped, x_codes, x_scales = {}, {}, {}, {}
        c_grouped, c_codes, c_scales = {}, {}, {}
        kv_banks = {}
        keys_sb, block_max, factors = {}, {}, {}

        def turn_x(n):
            x_turned[n] = turn(x_blocks[n], ps_turn, "turned")

        def regroup_x(n):
            grouped = stage.tile([P, BLOCK * PACK], BF16, align_bytes=64, tag="x_grouped")
            first = nc.scalar.copy if n == 0 else nc.vector.tensor_copy
            regroup(x_turned[n], grouped, (first, nc.vector.tensor_copy))
            x_grouped[n] = grouped

        def quantise_x(n):
            codes = stage.tile([P, BLOCK], U32, align_bytes=64, tag="x_codes")
            scales = stage.tile([P, BLOCK], U8, align_bytes=64, tag="x_scales")
            (quantise_halves if n == 0 else quantise)(x_grouped[n], codes, scales)
            x_codes[n], x_scales[n] = codes, scales

        def compress(n):
            grouped = stage.tile([P, BLOCK * PACK], BF16, align_bytes=64, tag="c_grouped")
            by_tile = grouped[:].rearrange("p (t r j) -> p t r j", t=TILES, j=PACK)
            for t in range(TILES):
                cols = slice(t * P, (t + 1) * P)
                bank = ps_kvc.tile([P, PACK, P], F32, tag="kvc")
                for j in range(PACK):
                    w_cols = slice(j * P, (j + 1) * P)
                    nc.tensor.matmul_mx(
                        out=bank[:, j, :],
                        lhsT=wc_codes[:, w_cols].bitcast(FP8X4),
                        lhsT_scale=wc_scales[:, w_cols],
                        rhs=x_codes[n][:, cols].bitcast(FP8X4),
                        rhs_scale=x_scales[n][:, cols],
                        start=True,
                        stop=True,
                    )
                shared = n == N_BLOCKS - 1 and t % 2 == 1
                copy = nc.vector.tensor_copy if shared else nc.scalar.copy
                copy(out=by_tile[:, t, :, :], in_=bank[:].rearrange("p j r -> p r j"))
            c_grouped[n] = grouped

        def quantise_c(n):
            codes = stage.tile([P, BLOCK], U32, align_bytes=64, tag="c_codes")
            scales = stage.tile([P, BLOCK], U8, align_bytes=64, tag="c_scales")
            (quantise_halves if n == N_BLOCKS - 1 else quantise)(c_grouped[n], codes, scales)
            c_codes[n], c_scales[n] = codes, scales

        def expand(n):
            kv_banks[n] = []
            for half in HALVES:
                pool, tag = (ps_kvc, "kvc") if n == N_BLOCKS - 1 else (ps_kv, "kv")
                bank = pool.tile([P, TILES // 2, 2, KEYS], F32, tag=tag)
                for t in range(half.start, half.stop):
                    cols = slice(t * P, (t + 1) * P)
                    nc.tensor.matmul_mx(
                        out=bank[:, t - half.start].rearrange("p s f -> p (s f)"),
                        lhsT=c_codes[n][:, cols].bitcast(FP8X4),
                        lhsT_scale=c_scales[n][:, cols],
                        rhs=wb_codes[:].bitcast(FP8X4),
                        rhs_scale=wb_scales[:],
                        start=True,
                        stop=True,
                    )
                kv_banks[n].append(bank)

        def leave_keys(n):
            b, rows = rows_of(n)
            if n % BLOCKS_PER_BATCH == 0:
                batch_keys = key_pool.tile([P, ROWS, KEYS], F32)
                keys_sb[b] = batch_keys
                maxima = small.tile([P, BLOCKS_PER_BATCH], F32)
                block_max[b] = maxima
            for bank, half in zip(kv_banks[n], HALVES):
                some = slice(rows.start + half.start, rows.start + half.stop)
                nc.scalar.activation(
                    out=keys_sb[b][:, some, :], in_=bank[:, :, 0, :], func=ACT.Silu
                )

        def leave_values(n):
            b, rows = rows_of(n)
            v_sb = val_pool.tile([P, TILES, KEYS], F32)
            to_vector = n % VECTOR_VALUES_EVERY == VECTOR_VALUES_EVERY // 2
            copy = nc.vector.tensor_copy if to_vector else nc.scalar.copy
            for bank, half in zip(kv_banks[n], HALVES):
                copy(out=v_sb[:, half, :], in_=bank[:, :, 1, :])
            nc.sync.dma_start(out=v_rows[b, :, rows, :], in_=v_sb[:])

        def maximum(n):
            b, rows = rows_of(n)
            place = n % BLOCKS_PER_BATCH
            nc.vector.tensor_reduce(
                out=block_max[b][:, place : place + 1],
                in_=keys_sb[b][:, rows, :].rearrange("p i f -> p (i f)"),
                axis=AXIS.X,
                op=ALU.max,
            )

        own_max, spread_banks = {}, {}

        def join_maxima(b):
            own = small.tile([P, 1], F32)
            nc.vector.tensor_reduce(out=own[:], in_=block_max[b][:], axis=AXIS.X, op=ALU.max)
            own_max[b] = own

        def spread_maxima(b):
            spread = ps_kv.tile([P, P], F32, tag="kv")
            nc.tensor.transpose(spread[:], own_max[b][:].to_broadcast([P, P]), ident[:])
            spread_banks[b] = spread

        def make_factors(b):
            group_max = small.tile([P, HEADS], F32)
            nc.vector.tensor_reduce(
                out=group_max[:],
                in_=spread_banks[b][:].rearrange("p (g q) -> p g q", g=HEADS),
                axis=AXIS.X,
                op=ALU.max,
            )
            divisor = small.tile([P, HEADS], F32)
            nc.vector.scalar_tensor_tensor(
                out=divisor[:], in0=group_max[:], scalar=0.0, in1=group_max[:],
                op0=ALU.is_equal, op1=ALU.add,
            )
            inverse = small.tile([P, HEADS], F32)
            nc.vector.reciprocal(out=inverse[:], in_=divisor[:])
            eta = small.tile([P, HEADS], F32)
            nc.vector.tensor_scalar(
                out=eta[:], in0=inverse[:], scalar1=10.0, scalar2=1.0, op0=ALU.mult, op1=ALU.min
            )
            factors[b] = eta

        def head_of(b, h):
            return keys_sb[b][:, :, h * HEAD_KEYS : (h + 1) * HEAD_KEYS], factors[b][:, h : h + 1]

        def scale_on_gpsimd(b, h):
            head, eta = head_of(b, h)
            nc.gpsimd.tensor_scalar(
                out=head, in0=head, scalar1=eta, scalar2=1.0, op0=ALU.mult, op1=ALU.mult
            )

        def scale_on_vector(b, h):
            head, eta = head_of(b, h)
            nc.vector.tensor_scalar(out=head, in0=head, scalar1=eta, scalar2=None, op0=ALU.mult)

        def scale_on_scalar(b, h):
            head, eta = head_of(b, h)
            nc.scalar.activation(out=head, in_=head, func=ACT.Copy, scale=eta)

        def store_keys(b):
            nc.sync.dma_start(out=k_rows[b], in_=keys_sb[b][:])

        def live(n):
            return 0 <= n < N_BLOCKS

        regroup(turn(wc_rows, ps_kvc, "kvc"), wc_grouped, (nc.vector.tensor_copy, nc.scalar.copy))
        quantise_halves(wc_grouped, wc_codes, wc_scales)
        turn_x(0)

        for t in range(N_BLOCKS + 4):
            late = t - 7
            new_factors = live(late) and late % HEADS == 0
            if live(t):
                regroup_x(t)
            if live(t - 2):
                quantise_c(t - 2)
            if live(t - 3):
                leave_keys(t - 3)
                leave_values(t - 3)
            if live(t - 1):
                compress(t - 1)
            if new_factors:
                spread_maxima(late // HEADS)
            if live(t + 1):
                turn_x(t + 1)
            if t == 0:
                turn_wkv_b()
            if live(t - 2):
                expand(t - 2)
            if live(t):
                quantise_x(t)
            if t == 1:
                quantise(wb_grouped, wb_codes, wb_scales)
            if new_factors:
                make_factors(late // HEADS)
            if live(t - 3):
                maximum(t - 3)
                if (t - 3) % BLOCKS_PER_BATCH == BLOCKS_PER_BATCH - 1:
                    join_maxima((t - 3) // BLOCKS_PER_BATCH)
            if live(late) and late // HEADS < BATCHES - 1:
                scale_on_gpsimd(late // HEADS, late % HEADS)
                if late % HEADS == HEADS - 1:
                    store_keys(late // HEADS)

        last = BATCHES - 1
        scale_on_vector(last, 0)
        scale_on_scalar(last, 2)
        scale_on_gpsimd(last, 3)
        scale_on_vector(last, 1)
        store_keys(last)
